import numpy as np
import ml_dtypes


def mxq(x, axis, fmt="e4m3"):
    dtype, down = {"e4m3": (ml_dtypes.float8_e4m3fn, 7), "e5m2": (ml_dtypes.float8_e5m2, 14)}[fmt]
    v = np.moveaxis(np.asarray(x, np.float32).astype(ml_dtypes.bfloat16).astype(np.float64), axis, -1)
    blocks = v.reshape(v.shape[:-1] + (-1, 32))
    amax = np.abs(blocks).max(-1, keepdims=True)
    byte = np.maximum(np.where(amax > 0, np.frexp(amax)[1] - 1 + 127, 0) - down, 1)
    scale = np.exp2(byte - 127.0)
    codes = (blocks / scale).astype(np.float32).astype(dtype).astype(np.float64)
    return np.moveaxis((codes * scale).reshape(v.shape), -1, axis)


WIDE = False


def mx_kscale(k):
    if not WIDE:
        return np.ones(k)
    levels = np.array([10, -10, 5, -5, 0])
    a = np.random.permutation(np.resize(levels, k // 512 * 4)).reshape(k // 512, 4)
    idx = np.arange(k)
    return np.exp2(a[idx // 512, idx % 128 // 32])


BF16 = ml_dtypes.bfloat16


def bf(x):
    return np.asarray(x, np.float32).astype(BF16)


def f64(x):
    return np.asarray(x).astype(np.float64)


B, T, U, D_ENC, D_PRED, D_JOINT, VOCAB = 4, 64, 32, 512, 512, 512, 1024
LOGIT_CLAMP = 15.0


def setup_inputs():
    se, sp = mx_kscale(D_ENC), mx_kscale(D_PRED)
    t = mx_kscale(D_JOINT)
    g = t / t.max()
    return {"encoder_out": bf(np.random.standard_normal((B, T, D_ENC)) * se),
            "predictor_out": bf(np.random.standard_normal((B, U, D_PRED)) * sp),
            "W_enc": bf(np.random.standard_normal((D_ENC, D_JOINT)) * 0.7 / np.sqrt(D_ENC) / se[:, None] * g),
            "b_enc": bf(np.random.standard_normal(D_JOINT) * 0.2 * g),
            "W_pred": bf(np.random.standard_normal((D_PRED, D_JOINT)) * 0.7 / np.sqrt(D_PRED) / sp[:, None] * g),
            "b_pred": bf(np.random.standard_normal(D_JOINT) * 0.2 * g),
            "W_out": bf(np.random.standard_normal((D_JOINT, VOCAB)) * 8.0 / np.sqrt(D_JOINT) / g[:, None]),
            "b_out": bf(np.random.standard_normal(VOCAB) * 0.5)}


def reference(encoder_out, predictor_out, W_enc, b_enc, W_pred, b_pred, W_out, b_out):
    enc = (mxq(f64(encoder_out), 2, "e4m3") @ mxq(f64(W_enc), 0, "e4m3")) + f64(b_enc)
    pred = (mxq(f64(predictor_out), 2, "e4m3") @ mxq(f64(W_pred), 0, "e4m3")) + f64(b_pred)
    joint = np.tanh(enc[:, :, None, :] + pred[:, None, :, :])
    logits = (mxq(joint, 3, "e4m3") @ mxq(f64(W_out), 0, "e4m3")) + f64(b_out)
    return np.clip(logits, -LOGIT_CLAMP, LOGIT_CLAMP)

@@ -1,0 +1,217 @@
+import concourse.mybir as mybir
+from concourse.masks import make_identity
+
+F32 = mybir.dt.float32
+BF16 = mybir.dt.bfloat16
+U32 = mybir.dt.uint32
+U8 = mybir.dt.uint8
+FP8X4 = mybir.dt.float8_e4m3fn_x4
+ADD = mybir.AluOpType.add
+MIN = mybir.AluOpType.min
+MAX = mybir.AluOpType.max
+TANH = mybir.ActivationFunctionType.Tanh
+
+P = 128
+PACK = 4
+BATCH, T_LEN, U_LEN = 4, 64, 32
+DIM = P * PACK
+VOCAB = 1024
+BANK = 512
+LOGIT_CLAMP = 15.0
+
+ENC_TOKENS = BATCH * T_LEN
+PRED_TOKENS = BATCH * U_LEN
+TOKEN_TILES = (ENC_TOKENS + PRED_TOKENS) // P
+T_STEP = 16
+ROUND_ROWS = T_STEP * U_LEN
+ROUNDS = BATCH * T_LEN // T_STEP
+ROW_TILES = ROUND_ROWS // P
+VOCAB_HALVES = VOCAB // BANK
+
+FLOPS = 2 * DIM * (ENC_TOKENS * DIM + PRED_TOKENS * DIM + BATCH * T_LEN * U_LEN * VOCAB)
+
+
+def load_k_first(nc, pool, weight, width, name):
+    raw = pool.tile([P, PACK, width], BF16, name=name)
+    nc.sync.dma_start(out=raw[:], in_=weight.rearrange("(t p) c -> p t c", p=P))
+    return raw
+
+
+def quantise(nc, grouped, codes, scales):
+    nc.vector.quantize_mx(
+        out=codes.bitcast(FP8X4),
+        scales=scales,
+        in_=grouped.rearrange("p c t -> p (c t)"),
+    )
+
+
+def tile_jointnetwork_kernel(
+    tc, encoder_out, predictor_out, W_enc, b_enc, W_pred, b_pred, W_out, b_out, out
+):
+    nc = tc.nc
+    out_rows = out.flatten_outer_dims()
+
+    with tc.tile_pool(name="keep", bufs=1) as keep:
+        tokens = keep.tile([P, TOKEN_TILES, DIM], BF16)
+        nc.sync.dma_start(
+            out=tokens[:, 0:2, :],
+            in_=encoder_out.flatten_outer_dims().rearrange("(n p) k -> p n k", p=P),
+        )
+        nc.sync.dma_start(out=tokens[:, 2, :], in_=predictor_out.flatten_outer_dims())
+        w_enc_raw = load_k_first(nc, keep, W_enc, DIM, "w_enc_raw")
+        w_pred_raw = load_k_first(nc, keep, W_pred, DIM, "w_pred_raw")
+        bias_rows = keep.tile([P, P], BF16)
+        nc.vector.memset(bias_rows[:], 0.0)
+        nc.scalar.dma_start(out=bias_rows[0:PACK, :], in_=b_enc.rearrange("(j p) -> j p", p=P))
+        nc.scalar.dma_start(
+            out=bias_rows[PACK : 2 * PACK, :], in_=b_pred.rearrange("(j p) -> j p", p=P)
+        )
+        w_out_raw = load_k_first(nc, keep, W_out, VOCAB, "w_out_raw")
+        b_out_bf16 = keep.tile([P, VOCAB], BF16)
+        nc.scalar.dma_start(out=b_out_bf16[:], in_=b_out.partition_broadcast(P))
+
+        identity = keep.tile([P, P], BF16)
+        make_identity(nc, identity[:])
+
+        token_codes = keep.tile([P, TOKEN_TILES * P], U32, align_bytes=64)
+        token_scales = keep.tile([P, TOKEN_TILES * P], U8, align_bytes=64)
+        w_enc_codes = keep.tile([P, DIM], U32, align_bytes=64)
+        w_enc_scales = keep.tile([P, DIM], U8, align_bytes=64)
+        w_pred_codes = keep.tile([P, DIM], U32, align_bytes=64)
+        w_pred_scales = keep.tile([P, DIM], U8, align_bytes=64)
+        w_out_codes = keep.tile([P, VOCAB], U32, align_bytes=64)
+        w_out_scales = keep.tile([P, VOCAB], U8, align_bytes=64)
+        projected = keep.tile([P, TOKEN_TILES * P, PACK], F32)
+        b_out_f32 = keep.tile([P, VOCAB], F32)
+
+        with tc.psum_pool(name="first_psum", bufs=2) as first_psum:
+            token_grouped = keep.tile([P, TOKEN_TILES * P, PACK], BF16, align_bytes=64)
+            for n in range(TOKEN_TILES):
+                flipped = first_psum.tile([P, PACK, P], BF16)
+                for t in range(PACK):
+                    nc.tensor.transpose(
+                        flipped[:, t, :], tokens[:, n, t * P : (t + 1) * P], identity[:]
+                    )
+                nc.scalar.copy(
+                    out=token_grouped[:, n * P : (n + 1) * P, :],
+                    in_=flipped[:].rearrange("p t r -> p r t"),
+                )
+            bias_flipped = first_psum.tile([P, P], BF16)
+            nc.tensor.transpose(bias_flipped[:], bias_rows[:], identity[:])
+            bias_columns = keep.tile([P, 2 * PACK], F32)
+            nc.scalar.copy(out=bias_columns[:], in_=bias_flipped[:, 0 : 2 * PACK])
+
+            w_enc_grouped = keep.tile([P, DIM, PACK], BF16, align_bytes=64)
+            nc.vector.tensor_copy(
+                out=w_enc_grouped[:], in_=w_enc_raw[:].rearrange("p t c -> p c t")
+            )
+            w_pred_grouped = keep.tile([P, DIM, PACK], BF16, align_bytes=64)
+            nc.vector.tensor_copy(
+                out=w_pred_grouped[:], in_=w_pred_raw[:].rearrange("p t c -> p c t")
+            )
+            quantise(
+                nc,
+                token_grouped[:, 0:ENC_TOKENS, :],
+                token_codes[:, 0:ENC_TOKENS],
+                token_scales[:, 0:ENC_TOKENS],
+            )
+            quantise(
+                nc,
+                token_grouped[:, ENC_TOKENS:, :],
+                token_codes[:, ENC_TOKENS:],
+                token_scales[:, ENC_TOKENS:],
+            )
+            quantise(nc, w_enc_grouped[:], w_enc_codes[:], w_enc_scales[:])
+            quantise(nc, w_pred_grouped[:], w_pred_codes[:], w_pred_scales[:])
+
+            for n in range(TOKEN_TILES):
+                is_encoder = n * P < ENC_TOKENS
+                codes = w_enc_codes if is_encoder else w_pred_codes
+                scales = w_enc_scales if is_encoder else w_pred_scales
+                bias = bias_columns[:, 0:PACK] if is_encoder else bias_columns[:, PACK:]
+                product = first_psum.tile([P, PACK, P], F32)
+                for j in range(PACK):
+                    nc.tensor.matmul_mx(
+                        out=product[:, j, :],
+                        lhsT=codes[:, j * P : (j + 1) * P].bitcast(FP8X4),
+                        lhsT_scale=scales[:, j * P : (j + 1) * P],
+                        rhs=token_codes[:, n * P : (n + 1) * P].bitcast(FP8X4),
+                        rhs_scale=token_scales[:, n * P : (n + 1) * P],
+                        start=True,
+                        stop=True,
+                    )
+                nc.vector.tensor_tensor(
+                    out=projected[:, n * P : (n + 1) * P, :],
+                    in0=product[:].rearrange("p j r -> p r j"),
+                    in1=bias.unsqueeze(1).to_broadcast([P, P, PACK]),
+                    op=ADD,
+                )
+
+            w_out_grouped = keep.tile([P, VOCAB, PACK], BF16, align_bytes=64)
+            nc.vector.tensor_copy(
+                out=w_out_grouped[:], in_=w_out_raw[:].rearrange("p t c -> p c t")
+            )
+            quantise(nc, w_out_grouped[:], w_out_codes[:], w_out_scales[:])
+            nc.vector.tensor_copy(out=b_out_f32[:], in_=b_out_bf16[:])
+
+        with (
+            tc.tile_pool(name="work", bufs=3) as work,
+            tc.tile_pool(name="logits", bufs=3) as logits_pool,
+            tc.psum_pool(name="acc_psum", bufs=8) as acc_psum,
+        ):
+            for r in range(ROUNDS):
+                b = r * T_STEP // T_LEN
+                enc_first = r * T_STEP
+                pred_first = ENC_TOKENS + b * U_LEN
+                shape = [P, T_STEP, U_LEN, PACK]
+
+                summed = work.tile(shape, F32)
+                nc.vector.tensor_tensor(
+                    out=summed[:],
+                    in0=projected[:, enc_first : enc_first + T_STEP, :]
+                    .unsqueeze(2)
+                    .to_broadcast(shape),
+                    in1=projected[:, pred_first : pred_first + U_LEN, :]
+                    .unsqueeze(1)
+                    .to_broadcast(shape),
+                    op=ADD,
+                )
+                joint = work.tile([P, ROUND_ROWS, PACK], BF16, align_bytes=64)
+                nc.scalar.activation(
+                    out=joint[:], in_=summed[:].rearrange("p t u j -> p (t u) j"), func=TANH
+                )
+                joint_codes = work.tile([P, ROUND_ROWS], U32, align_bytes=64)
+                joint_scales = work.tile([P, ROUND_ROWS], U8, align_bytes=64)
+                quantise(nc, joint[:], joint_codes[:], joint_scales[:])
+
+                logits = logits_pool.tile([P, ROW_TILES, VOCAB], F32)
+                for m in range(ROW_TILES):
+                    for h in range(VOCAB_HALVES):
+                        acc = acc_psum.tile([P, BANK], F32)
+                        nc.tensor.matmul_mx(
+                            out=acc[:],
+                            lhsT=joint_codes[:, m * P : (m + 1) * P].bitcast(FP8X4),
+                            lhsT_scale=joint_scales[:, m * P : (m + 1) * P],
+                            rhs=w_out_codes[:, h * BANK : (h + 1) * BANK].bitcast(FP8X4),
+                            rhs_scale=w_out_scales[:, h * BANK : (h + 1) * BANK],
+                            start=True,
+                            stop=True,
+                        )
+                        nc.vector.tensor_tensor(
+                            out=logits[:, m, h * BANK : (h + 1) * BANK],
+                            in0=acc[:],
+                            in1=b_out_f32[:, h * BANK : (h + 1) * BANK],
+                            op=ADD,
+                        )
+                    nc.gpsimd.tensor_scalar(
+                        out=logits[:, m, :],
+                        in0=logits[:, m, :],
+                        scalar1=LOGIT_CLAMP,
+                        scalar2=-LOGIT_CLAMP,
+                        op0=MIN,
+                        op1=MAX,
+                    )
+                    first_row = r * ROUND_ROWS + m * P
+                    nc.sync.dma_start(
+                        out=out_rows[first_row : first_row + P, :], in_=logits[:, m, :]
+                    )

@@ -27,6 +27,7 @@ ROUND_ROWS = T_STEP * U_LEN
 ROUNDS = BATCH * T_LEN // T_STEP
 ROW_TILES = ROUND_ROWS // P
 VOCAB_HALVES = VOCAB // BANK
+BANKS = ROW_TILES * VOCAB_HALVES
 
 FLOPS = 2 * DIM * (ENC_TOKENS * DIM + PRED_TOKENS * DIM + BATCH * T_LEN * U_LEN * VOCAB)
 
@@ -157,15 +158,19 @@ def tile_jointnetwork_kernel(
         with (
             tc.tile_pool(name="work", bufs=3) as work,
             tc.tile_pool(name="logits", bufs=3) as logits_pool,
-            tc.psum_pool(name="acc_psum", bufs=8) as acc_psum,
+            tc.psum_pool(name="acc_psum", bufs=BANKS) as acc_psum,
         ):
-            for r in range(ROUNDS):
+            joint_of = {}
+            codes_of = {}
+            acc_of = {}
+            logits_of = {}
+
+            def form_joint(r):
                 b = r * T_STEP // T_LEN
                 enc_first = r * T_STEP
                 pred_first = ENC_TOKENS + b * U_LEN
                 shape = [P, T_STEP, U_LEN, PACK]
-
-                summed = work.tile(shape, F32)
+                summed = work.tile(shape, F32, name="summed")
                 nc.vector.tensor_tensor(
                     out=summed[:],
                     in0=projected[:, enc_first : enc_first + T_STEP, :]
@@ -176,42 +181,70 @@ def tile_jointnetwork_kernel(
                     .to_broadcast(shape),
                     op=ADD,
                 )
-                joint = work.tile([P, ROUND_ROWS, PACK], BF16, align_bytes=64)
+                joint = work.tile([P, ROUND_ROWS, PACK], BF16, align_bytes=64, name="joint")
                 nc.scalar.activation(
                     out=joint[:], in_=summed[:].rearrange("p t u j -> p (t u) j"), func=TANH
                 )
-                joint_codes = work.tile([P, ROUND_ROWS], U32, align_bytes=64)
-                joint_scales = work.tile([P, ROUND_ROWS], U8, align_bytes=64)
-                quantise(nc, joint[:], joint_codes[:], joint_scales[:])
+                joint_of[r] = joint
 
-                logits = logits_pool.tile([P, ROW_TILES, VOCAB], F32)
-                for m in range(ROW_TILES):
-                    for h in range(VOCAB_HALVES):
-                        acc = acc_psum.tile([P, BANK], F32)
-                        nc.tensor.matmul_mx(
-                            out=acc[:],
-                            lhsT=joint_codes[:, m * P : (m + 1) * P].bitcast(FP8X4),
-                            lhsT_scale=joint_scales[:, m * P : (m + 1) * P],
-                            rhs=w_out_codes[:, h * BANK : (h + 1) * BANK].bitcast(FP8X4),
-                            rhs_scale=w_out_scales[:, h * BANK : (h + 1) * BANK],
-                            start=True,
-                            stop=True,
-                        )
-                        nc.vector.tensor_tensor(
-                            out=logits[:, m, h * BANK : (h + 1) * BANK],
-                            in0=acc[:],
-                            in1=b_out_f32[:, h * BANK : (h + 1) * BANK],
-                            op=ADD,
-                        )
-                    nc.gpsimd.tensor_scalar(
-                        out=logits[:, m, :],
-                        in0=logits[:, m, :],
-                        scalar1=LOGIT_CLAMP,
-                        scalar2=-LOGIT_CLAMP,
-                        op0=MIN,
-                        op1=MAX,
-                    )
-                    first_row = r * ROUND_ROWS + m * P
-                    nc.sync.dma_start(
-                        out=out_rows[first_row : first_row + P, :], in_=logits[:, m, :]
-                    )
+            def quantise_joint(r):
+                codes = work.tile([P, ROUND_ROWS], U32, align_bytes=64, name="joint_codes")
+                scales = work.tile([P, ROUND_ROWS], U8, align_bytes=64, name="joint_scales")
+                quantise(nc, joint_of[r][:], codes[:], scales[:])
+                codes_of[r] = (codes, scales)
+
+            def multiply(r, bank):
+                m, h = bank // VOCAB_HALVES, bank % VOCAB_HALVES
+                codes, scales = codes_of[r]
+                acc = acc_psum.tile([P, BANK], F32, name="acc")
+                nc.tensor.matmul_mx(
+                    out=acc[:],
+                    lhsT=codes[:, m * P : (m + 1) * P].bitcast(FP8X4),
+                    lhsT_scale=scales[:, m * P : (m + 1) * P],
+                    rhs=w_out_codes[:, h * BANK : (h + 1) * BANK].bitcast(FP8X4),
+                    rhs_scale=w_out_scales[:, h * BANK : (h + 1) * BANK],
+                    start=True,
+                    stop=True,
+                )
+                acc_of[(r, bank)] = acc
+
+            def add_bias(r, bank):
+                m, h = bank // VOCAB_HALVES, bank % VOCAB_HALVES
+                nc.vector.tensor_tensor(
+                    out=logits_of[r][:, m, h * BANK : (h + 1) * BANK],
+                    in0=acc_of[(r, bank)][:],
+                    in1=b_out_f32[:, h * BANK : (h + 1) * BANK],
+                    op=ADD,
+                )
+
+            def clamp_and_store(r, m):
+                rows = logits_of[r][:, m, :]
+                nc.gpsimd.tensor_scalar(
+                    out=rows,
+                    in0=rows,
+                    scalar1=LOGIT_CLAMP,
+                    scalar2=-LOGIT_CLAMP,
+                    op0=MIN,
+                    op1=MAX,
+                )
+                first_row = r * ROUND_ROWS + m * P
+                nc.sync.dma_start(out=out_rows[first_row : first_row + P, :], in_=rows)
+
+            with tc.manual_schedule():
+                form_joint(0)
+                form_joint(1)
+                quantise_joint(0)
+                for bank in range(BANKS):
+                    multiply(0, bank)
+                for r in range(ROUNDS):
+                    if r + 2 < ROUNDS:
+                        form_joint(r + 2)
+                    if r + 1 < ROUNDS:
+                        quantise_joint(r + 1)
+                    logits_of[r] = logits_pool.tile([P, ROW_TILES, VOCAB], F32, name="logits")
+                    for bank in range(BANKS):
+                        add_bias(r, bank)
+                        if r + 1 < ROUNDS:
+                            multiply(r + 1, bank)
+                        if bank % VOCAB_HALVES == VOCAB_HALVES - 1:
+                            clamp_and_store(r, bank // VOCAB_HALVES)

@@ -171,7 +171,7 @@ def tile_jointnetwork_kernel(
                 pred_first = ENC_TOKENS + b * U_LEN
                 shape = [P, T_STEP, U_LEN, PACK]
                 summed = work.tile(shape, F32, name="summed")
-                nc.vector.tensor_tensor(
+                nc.gpsimd.tensor_tensor(
                     out=summed[:],
                     in0=projected[:, enc_first : enc_first + T_STEP, :]
                     .unsqueeze(2)
@@ -219,7 +219,7 @@ def tile_jointnetwork_kernel(
 
             def clamp_and_store(r, m):
                 rows = logits_of[r][:, m, :]
-                nc.gpsimd.tensor_scalar(
+                nc.vector.tensor_scalar(
                     out=rows,
                     in0=rows,
                     scalar1=LOGIT_CLAMP,
@@ -242,9 +242,14 @@ def tile_jointnetwork_kernel(
                     if r + 1 < ROUNDS:
                         quantise_joint(r + 1)
                     logits_of[r] = logits_pool.tile([P, ROW_TILES, VOCAB], F32, name="logits")
-                    for bank in range(BANKS):
-                        add_bias(r, bank)
-                        if r + 1 < ROUNDS:
-                            multiply(r + 1, bank)
-                        if bank % VOCAB_HALVES == VOCAB_HALVES - 1:
-                            clamp_and_store(r, bank // VOCAB_HALVES)
+                    for m in range(ROW_TILES):
+                        for h in range(VOCAB_HALVES):
+                            bank = m * VOCAB_HALVES + h
+                            add_bias(r, bank)
+                            if r + 1 < ROUNDS:
+                                multiply(r + 1, bank)
+                        if m > 0:
+                            clamp_and_store(r, m - 1)
+                        elif r > 0:
+                            clamp_and_store(r - 1, ROW_TILES - 1)
+                clamp_and_store(ROUNDS - 1, ROW_TILES - 1)

@@ -10,6 +10,7 @@ ADD = mybir.AluOpType.add
 MIN = mybir.AluOpType.min
 MAX = mybir.AluOpType.max
 TANH = mybir.ActivationFunctionType.Tanh
+IDENTITY = mybir.ActivationFunctionType.Identity
 
 P = 128
 PACK = 4
@@ -26,8 +27,10 @@ T_STEP = 16
 ROUND_ROWS = T_STEP * U_LEN
 ROUNDS = BATCH * T_LEN // T_STEP
 ROW_TILES = ROUND_ROWS // P
+VOCAB_BLOCKS = VOCAB // P
+BLOCKS_IN_BANK = BANK // P
 VOCAB_HALVES = VOCAB // BANK
-BANKS = ROW_TILES * VOCAB_HALVES
+HALF_OF_PSUM = 4
 
 FLOPS = 2 * DIM * (ENC_TOKENS * DIM + PRED_TOKENS * DIM + BATCH * T_LEN * U_LEN * VOCAB)
 
@@ -63,16 +66,20 @@ def tile_jointnetwork_kernel(
         w_pred_raw = load_k_first(nc, keep, W_pred, DIM, "w_pred_raw")
         bias_rows = keep.tile([P, P], BF16)
         nc.vector.memset(bias_rows[:], 0.0)
-        nc.scalar.dma_start(out=bias_rows[0:PACK, :], in_=b_enc.rearrange("(j p) -> j p", p=P))
-        nc.scalar.dma_start(
-            out=bias_rows[PACK : 2 * PACK, :], in_=b_pred.rearrange("(j p) -> j p", p=P)
-        )
+        first_bias_row = 0
+        for bias in (b_enc, b_pred, b_out):
+            rows = bias.shape[0] // P
+            nc.scalar.dma_start(
+                out=bias_rows[first_bias_row : first_bias_row + rows, :],
+                in_=bias.rearrange("(j p) -> j p", p=P),
+            )
+            first_bias_row += rows
         w_out_raw = load_k_first(nc, keep, W_out, VOCAB, "w_out_raw")
-        b_out_bf16 = keep.tile([P, VOCAB], BF16)
-        nc.scalar.dma_start(out=b_out_bf16[:], in_=b_out.partition_broadcast(P))
 
-        identity = keep.tile([P, P], BF16)
-        make_identity(nc, identity[:])
+        identity_bf16 = keep.tile([P, P], BF16)
+        make_identity(nc, identity_bf16[:])
+        identity_f32 = keep.tile([P, P], F32)
+        make_identity(nc, identity_f32[:])
 
         token_codes = keep.tile([P, TOKEN_TILES * P], U32, align_bytes=64)
         token_scales = keep.tile([P, TOKEN_TILES * P], U8, align_bytes=64)
@@ -83,7 +90,10 @@ def tile_jointnetwork_kernel(
         w_out_codes = keep.tile([P, VOCAB], U32, align_bytes=64)
         w_out_scales = keep.tile([P, VOCAB], U8, align_bytes=64)
         projected = keep.tile([P, TOKEN_TILES * P, PACK], F32)
-        b_out_f32 = keep.tile([P, VOCAB], F32)
+        bias_columns = keep.tile([P, 2 * PACK + VOCAB_BLOCKS], F32)
+        b_enc_columns = bias_columns[:, 0:PACK]
+        b_pred_columns = bias_columns[:, PACK : 2 * PACK]
+        b_out_columns = bias_columns[:, 2 * PACK :]
 
         with tc.psum_pool(name="first_psum", bufs=2) as first_psum:
             token_grouped = keep.tile([P, TOKEN_TILES * P, PACK], BF16, align_bytes=64)
@@ -91,16 +101,15 @@ def tile_jointnetwork_kernel(
                 flipped = first_psum.tile([P, PACK, P], BF16)
                 for t in range(PACK):
                     nc.tensor.transpose(
-                        flipped[:, t, :], tokens[:, n, t * P : (t + 1) * P], identity[:]
+                        flipped[:, t, :], tokens[:, n, t * P : (t + 1) * P], identity_bf16[:]
                     )
                 nc.scalar.copy(
                     out=token_grouped[:, n * P : (n + 1) * P, :],
                     in_=flipped[:].rearrange("p t r -> p r t"),
                 )
             bias_flipped = first_psum.tile([P, P], BF16)
-            nc.tensor.transpose(bias_flipped[:], bias_rows[:], identity[:])
-            bias_columns = keep.tile([P, 2 * PACK], F32)
-            nc.scalar.copy(out=bias_columns[:], in_=bias_flipped[:, 0 : 2 * PACK])
+            nc.tensor.transpose(bias_flipped[:], bias_rows[:], identity_bf16[:])
+            nc.scalar.copy(out=bias_columns[:], in_=bias_flipped[:, 0 : 2 * PACK + VOCAB_BLOCKS])
 
             w_enc_grouped = keep.tile([P, DIM, PACK], BF16, align_bytes=64)
             nc.vector.tensor_copy(
@@ -129,7 +138,7 @@ def tile_jointnetwork_kernel(
                 is_encoder = n * P < ENC_TOKENS
                 codes = w_enc_codes if is_encoder else w_pred_codes
                 scales = w_enc_scales if is_encoder else w_pred_scales
-                bias = bias_columns[:, 0:PACK] if is_encoder else bias_columns[:, PACK:]
+                bias = b_enc_columns if is_encoder else b_pred_columns
                 product = first_psum.tile([P, PACK, P], F32)
                 for j in range(PACK):
                     nc.tensor.matmul_mx(
@@ -153,26 +162,26 @@ def tile_jointnetwork_kernel(
                 out=w_out_grouped[:], in_=w_out_raw[:].rearrange("p t c -> p c t")
             )
             quantise(nc, w_out_grouped[:], w_out_codes[:], w_out_scales[:])
-            nc.vector.tensor_copy(out=b_out_f32[:], in_=b_out_bf16[:])
 
         with (
             tc.tile_pool(name="work", bufs=3) as work,
-            tc.tile_pool(name="logits", bufs=3) as logits_pool,
-            tc.psum_pool(name="acc_psum", bufs=BANKS) as acc_psum,
+            tc.tile_pool(name="wide", bufs=3) as wide,
+            tc.psum_pool(name="psum", bufs=HALF_OF_PSUM) as psum,
         ):
+            summed_of = {}
             joint_of = {}
             codes_of = {}
-            acc_of = {}
+            biased_of = {}
             logits_of = {}
 
-            def form_joint(r):
+            def form_sum(r):
                 b = r * T_STEP // T_LEN
                 enc_first = r * T_STEP
                 pred_first = ENC_TOKENS + b * U_LEN
                 shape = [P, T_STEP, U_LEN, PACK]
-                summed = work.tile(shape, F32, name="summed")
-                nc.gpsimd.tensor_tensor(
-                    out=summed[:],
+                summed_of[r] = work.tile(shape, F32, name="summed")
+                nc.vector.tensor_tensor(
+                    out=summed_of[r][:],
                     in0=projected[:, enc_first : enc_first + T_STEP, :]
                     .unsqueeze(2)
                     .to_broadcast(shape),
@@ -181,11 +190,14 @@ def tile_jointnetwork_kernel(
                     .to_broadcast(shape),
                     op=ADD,
                 )
-                joint = work.tile([P, ROUND_ROWS, PACK], BF16, align_bytes=64, name="joint")
+
+            def take_tanh(r):
+                joint_of[r] = work.tile([P, ROUND_ROWS, PACK], BF16, align_bytes=64, name="joint")
                 nc.scalar.activation(
-                    out=joint[:], in_=summed[:].rearrange("p t u j -> p (t u) j"), func=TANH
+                    out=joint_of[r][:],
+                    in_=summed_of[r][:].rearrange("p t u j -> p (t u) j"),
+                    func=TANH,
                 )
-                joint_of[r] = joint
 
             def quantise_joint(r):
                 codes = work.tile([P, ROUND_ROWS], U32, align_bytes=64, name="joint_codes")
@@ -193,63 +205,82 @@ def tile_jointnetwork_kernel(
                 quantise(nc, joint_of[r][:], codes[:], scales[:])
                 codes_of[r] = (codes, scales)
 
-            def multiply(r, bank):
-                m, h = bank // VOCAB_HALVES, bank % VOCAB_HALVES
+            def project(r, half):
+                if half == 0:
+                    biased_of[r] = wide.tile([P, VOCAB_BLOCKS, ROUND_ROWS], F32, name="biased")
                 codes, scales = codes_of[r]
-                acc = acc_psum.tile([P, BANK], F32, name="acc")
-                nc.tensor.matmul_mx(
-                    out=acc[:],
-                    lhsT=codes[:, m * P : (m + 1) * P].bitcast(FP8X4),
-                    lhsT_scale=scales[:, m * P : (m + 1) * P],
-                    rhs=w_out_codes[:, h * BANK : (h + 1) * BANK].bitcast(FP8X4),
-                    rhs_scale=w_out_scales[:, h * BANK : (h + 1) * BANK],
-                    start=True,
-                    stop=True,
-                )
-                acc_of[(r, bank)] = acc
+                blocks = range(half * BLOCKS_IN_BANK, (half + 1) * BLOCKS_IN_BANK)
+                products = {}
+                for c in blocks:
+                    products[c] = psum.tile([P, ROUND_ROWS], F32, name="product")
+                    nc.tensor.matmul_mx(
+                        out=products[c][:],
+                        lhsT=w_out_codes[:, c * P : (c + 1) * P].bitcast(FP8X4),
+                        lhsT_scale=w_out_scales[:, c * P : (c + 1) * P],
+                        rhs=codes[:].bitcast(FP8X4),
+                        rhs_scale=scales[:],
+                        start=True,
+                        stop=True,
+                    )
+                for c in blocks:
+                    nc.scalar.activation(
+                        out=biased_of[r][:, c, :],
+                        in_=products[c][:],
+                        func=IDENTITY,
+                        bias=b_out_columns[:, c : c + 1],
+                    )
 
-            def add_bias(r, bank):
-                m, h = bank // VOCAB_HALVES, bank % VOCAB_HALVES
-                nc.vector.tensor_tensor(
-                    out=logits_of[r][:, m, h * BANK : (h + 1) * BANK],
-                    in0=acc_of[(r, bank)][:],
-                    in1=b_out_f32[:, h * BANK : (h + 1) * BANK],
-                    op=ADD,
-                )
+            def turn_back(r, m):
+                turned = []
+                for h in range(VOCAB_HALVES):
+                    bank = psum.tile([P, BLOCKS_IN_BANK, P], F32, name="turned")
+                    for i in range(BLOCKS_IN_BANK):
+                        nc.tensor.transpose(
+                            bank[:, i, :],
+                            biased_of[r][:, h * BLOCKS_IN_BANK + i, m * P : (m + 1) * P],
+                            identity_f32[:],
+                        )
+                    turned.append(bank)
+                return turned
 
-            def clamp_and_store(r, m):
-                rows = logits_of[r][:, m, :]
-                nc.vector.tensor_scalar(
-                    out=rows,
-                    in0=rows,
-                    scalar1=LOGIT_CLAMP,
-                    scalar2=-LOGIT_CLAMP,
-                    op0=MIN,
-                    op1=MAX,
-                )
+            def clamp_and_store(r, m, turned):
+                if m == 0:
+                    logits_of[r] = wide.tile([P, ROW_TILES, VOCAB], F32, name="logits")
+                for h in range(VOCAB_HALVES):
+                    nc.vector.tensor_scalar(
+                        out=logits_of[r][:, m, h * BANK : (h + 1) * BANK],
+                        in0=turned[h][:].rearrange("p i v -> p (i v)"),
+                        scalar1=LOGIT_CLAMP,
+                        scalar2=-LOGIT_CLAMP,
+                        op0=MIN,
+                        op1=MAX,
+                    )
                 first_row = r * ROUND_ROWS + m * P
-                nc.sync.dma_start(out=out_rows[first_row : first_row + P, :], in_=rows)
+                nc.sync.dma_start(
+                    out=out_rows[first_row : first_row + P, :], in_=logits_of[r][:, m, :]
+                )
 
             with tc.manual_schedule():
-                form_joint(0)
-                form_joint(1)
+                for r in range(3):
+                    form_sum(r)
+                    take_tanh(r)
                 quantise_joint(0)
-                for bank in range(BANKS):
-                    multiply(0, bank)
+                quantise_joint(1)
+                project(0, 0)
+                project(0, 1)
                 for r in range(ROUNDS):
+                    if r + 3 < ROUNDS:
+                        form_sum(r + 3)
                     if r + 2 < ROUNDS:
-                        form_joint(r + 2)
-                    if r + 1 < ROUNDS:
-                        quantise_joint(r + 1)
-                    logits_of[r] = logits_pool.tile([P, ROW_TILES, VOCAB], F32, name="logits")
-                    for m in range(ROW_TILES):
-                        for h in range(VOCAB_HALVES):
-                            bank = m * VOCAB_HALVES + h
-                            add_bias(r, bank)
-                            if r + 1 < ROUNDS:
-                                multiply(r + 1, bank)
-                        if m > 0:
-                            clamp_and_store(r, m - 1)
-                        elif r > 0:
-                            clamp_and_store(r - 1, ROW_TILES - 1)
-                clamp_and_store(ROUNDS - 1, ROW_TILES - 1)
+                        quantise_joint(r + 2)
+                    for half in range(VOCAB_HALVES):
+                        if r + 1 < ROUNDS:
+                            project(r + 1, half)
+                        if half == 0 and r + 3 < ROUNDS:
+                            take_tanh(r + 3)
+                        row_tiles = range(half * 2, half * 2 + 2)
+                        turned_of = {}
+                        for m in row_tiles:
+                            turned_of[m] = turn_back(r, m)
+                        for m in row_tiles:
+                            clamp_and_store(r, m, turned_of[m])

@@ -31,6 +31,7 @@ VOCAB_BLOCKS = VOCAB // P
 BLOCKS_IN_BANK = BANK // P
 VOCAB_HALVES = VOCAB // BANK
 HALF_OF_PSUM = 4
+T_ON_VECTOR = 12
 
 FLOPS = 2 * DIM * (ENC_TOKENS * DIM + PRED_TOKENS * DIM + BATCH * T_LEN * U_LEN * VOCAB)
 
@@ -178,18 +179,22 @@ def tile_jointnetwork_kernel(
                 b = r * T_STEP // T_LEN
                 enc_first = r * T_STEP
                 pred_first = ENC_TOKENS + b * U_LEN
-                shape = [P, T_STEP, U_LEN, PACK]
-                summed_of[r] = work.tile(shape, F32, name="summed")
-                nc.vector.tensor_tensor(
-                    out=summed_of[r][:],
-                    in0=projected[:, enc_first : enc_first + T_STEP, :]
-                    .unsqueeze(2)
-                    .to_broadcast(shape),
-                    in1=projected[:, pred_first : pred_first + U_LEN, :]
-                    .unsqueeze(1)
-                    .to_broadcast(shape),
-                    op=ADD,
-                )
+                summed_of[r] = work.tile([P, T_STEP, U_LEN, PACK], F32, name="summed")
+                for engine, first, last in (
+                    (nc.vector, 0, T_ON_VECTOR),
+                    (nc.gpsimd, T_ON_VECTOR, T_STEP),
+                ):
+                    shape = [P, last - first, U_LEN, PACK]
+                    engine.tensor_tensor(
+                        out=summed_of[r][:, first:last, :, :],
+                        in0=projected[:, enc_first + first : enc_first + last, :]
+                        .unsqueeze(2)
+                        .to_broadcast(shape),
+                        in1=projected[:, pred_first : pred_first + U_LEN, :]
+                        .unsqueeze(1)
+                        .to_broadcast(shape),
+                        op=ADD,
+                    )
 
             def take_tanh(r):
                 joint_of[r] = work.tile([P, ROUND_ROWS, PACK], BF16, align_bytes=64, name="joint")

@@ -31,7 +31,8 @@ VOCAB_BLOCKS = VOCAB // P
 BLOCKS_IN_BANK = BANK // P
 VOCAB_HALVES = VOCAB // BANK
 HALF_OF_PSUM = 4
-T_ON_VECTOR = 12
+T_ON_VECTOR = 8
+BLOCKS_ON_SCALAR = 7
 
 FLOPS = 2 * DIM * (ENC_TOKENS * DIM + PRED_TOKENS * DIM + BATCH * T_LEN * U_LEN * VOCAB)
 
@@ -228,12 +229,21 @@ def tile_jointnetwork_kernel(
                         stop=True,
                     )
                 for c in blocks:
-                    nc.scalar.activation(
-                        out=biased_of[r][:, c, :],
-                        in_=products[c][:],
-                        func=IDENTITY,
-                        bias=b_out_columns[:, c : c + 1],
-                    )
+                    if c < BLOCKS_ON_SCALAR:
+                        nc.scalar.activation(
+                            out=biased_of[r][:, c, :],
+                            in_=products[c][:],
+                            func=IDENTITY,
+                            bias=b_out_columns[:, c : c + 1],
+                        )
+                    else:
+                        nc.vector.tensor_scalar(
+                            out=biased_of[r][:, c, :],
+                            in0=products[c][:],
+                            scalar1=b_out_columns[:, c : c + 1],
+                            scalar2=None,
+                            op0=ADD,
+                        )
 
             def turn_back(r, m):
                 turned = []

import concourse.mybir as mybir
from concourse.masks import make_identity

F32 = mybir.dt.float32
BF16 = mybir.dt.bfloat16
U32 = mybir.dt.uint32
U8 = mybir.dt.uint8
FP8X4 = mybir.dt.float8_e4m3fn_x4
ADD = mybir.AluOpType.add
MIN = mybir.AluOpType.min
MAX = mybir.AluOpType.max
TANH = mybir.ActivationFunctionType.Tanh
IDENTITY = mybir.ActivationFunctionType.Identity

P = 128
PACK = 4
BATCH, T_LEN, U_LEN = 4, 64, 32
DIM = P * PACK
VOCAB = 1024
BANK = 512
LOGIT_CLAMP = 15.0

ENC_TOKENS = BATCH * T_LEN
PRED_TOKENS = BATCH * U_LEN
TOKEN_TILES = (ENC_TOKENS + PRED_TOKENS) // P
T_STEP = 16
ROUND_ROWS = T_STEP * U_LEN
ROUNDS = BATCH * T_LEN // T_STEP
ROW_TILES = ROUND_ROWS // P
VOCAB_BLOCKS = VOCAB // P
BLOCKS_IN_BANK = BANK // P
VOCAB_HALVES = VOCAB // BANK
HALF_OF_PSUM = 4
T_ON_VECTOR = 8
BLOCKS_ON_SCALAR = 7

FLOPS = 2 * DIM * (ENC_TOKENS * DIM + PRED_TOKENS * DIM + BATCH * T_LEN * U_LEN * VOCAB)


def load_k_first(nc, pool, weight, width, name):
    raw = pool.tile([P, PACK, width], BF16, name=name)
    nc.sync.dma_start(out=raw[:], in_=weight.rearrange("(t p) c -> p t c", p=P))
    return raw


def quantise(nc, grouped, codes, scales):
    nc.vector.quantize_mx(
        out=codes.bitcast(FP8X4),
        scales=scales,
        in_=grouped.rearrange("p c t -> p (c t)"),
    )


def tile_jointnetwork_kernel(
    tc, encoder_out, predictor_out, W_enc, b_enc, W_pred, b_pred, W_out, b_out, out
):
    nc = tc.nc
    out_rows = out.flatten_outer_dims()

    with tc.tile_pool(name="keep", bufs=1) as keep:
        tokens = keep.tile([P, TOKEN_TILES, DIM], BF16)
        nc.sync.dma_start(
            out=tokens[:, 0:2, :],
            in_=encoder_out.flatten_outer_dims().rearrange("(n p) k -> p n k", p=P),
        )
        nc.sync.dma_start(out=tokens[:, 2, :], in_=predictor_out.flatten_outer_dims())
        w_enc_raw = load_k_first(nc, keep, W_enc, DIM, "w_enc_raw")
        w_pred_raw = load_k_first(nc, keep, W_pred, DIM, "w_pred_raw")
        bias_rows = keep.tile([P, P], BF16)
        nc.vector.memset(bias_rows[:], 0.0)
        first_bias_row = 0
        for bias in (b_enc, b_pred, b_out):
            rows = bias.shape[0] // P
            nc.scalar.dma_start(
                out=bias_rows[first_bias_row : first_bias_row + rows, :],
                in_=bias.rearrange("(j p) -> j p", p=P),
            )
            first_bias_row += rows
        w_out_raw = load_k_first(nc, keep, W_out, VOCAB, "w_out_raw")

        identity_bf16 = keep.tile([P, P], BF16)
        make_identity(nc, identity_bf16[:])
        identity_f32 = keep.tile([P, P], F32)
        make_identity(nc, identity_f32[:])

        token_codes = keep.tile([P, TOKEN_TILES * P], U32, align_bytes=64)
        token_scales = keep.tile([P, TOKEN_TILES * P], U8, align_bytes=64)
        w_enc_codes = keep.tile([P, DIM], U32, align_bytes=64)
        w_enc_scales = keep.tile([P, DIM], U8, align_bytes=64)
        w_pred_codes = keep.tile([P, DIM], U32, align_bytes=64)
        w_pred_scales = keep.tile([P, DIM], U8, align_bytes=64)
        w_out_codes = keep.tile([P, VOCAB], U32, align_bytes=64)
        w_out_scales = keep.tile([P, VOCAB], U8, align_bytes=64)
        projected = keep.tile([P, TOKEN_TILES * P, PACK], F32)
        bias_columns = keep.tile([P, 2 * PACK + VOCAB_BLOCKS], F32)
        b_enc_columns = bias_columns[:, 0:PACK]
        b_pred_columns = bias_columns[:, PACK : 2 * PACK]
        b_out_columns = bias_columns[:, 2 * PACK :]

        with tc.psum_pool(name="first_psum", bufs=2) as first_psum:
            token_grouped = keep.tile([P, TOKEN_TILES * P, PACK], BF16, align_bytes=64)
            for n in range(TOKEN_TILES):
                flipped = first_psum.tile([P, PACK, P], BF16)
                for t in range(PACK):
                    nc.tensor.transpose(
                        flipped[:, t, :], tokens[:, n, t * P : (t + 1) * P], identity_bf16[:]
                    )
                nc.scalar.copy(
                    out=token_grouped[:, n * P : (n + 1) * P, :],
                    in_=flipped[:].rearrange("p t r -> p r t"),
                )
            bias_flipped = first_psum.tile([P, P], BF16)
            nc.tensor.transpose(bias_flipped[:], bias_rows[:], identity_bf16[:])
            nc.scalar.copy(out=bias_columns[:], in_=bias_flipped[:, 0 : 2 * PACK + VOCAB_BLOCKS])

            w_enc_grouped = keep.tile([P, DIM, PACK], BF16, align_bytes=64)
            nc.vector.tensor_copy(
                out=w_enc_grouped[:], in_=w_enc_raw[:].rearrange("p t c -> p c t")
            )
            w_pred_grouped = keep.tile([P, DIM, PACK], BF16, align_bytes=64)
            nc.vector.tensor_copy(
                out=w_pred_grouped[:], in_=w_pred_raw[:].rearrange("p t c -> p c t")
            )
            quantise(
                nc,
                token_grouped[:, 0:ENC_TOKENS, :],
                token_codes[:, 0:ENC_TOKENS],
                token_scales[:, 0:ENC_TOKENS],
            )
            quantise(
                nc,
                token_grouped[:, ENC_TOKENS:, :],
                token_codes[:, ENC_TOKENS:],
                token_scales[:, ENC_TOKENS:],
            )
            quantise(nc, w_enc_grouped[:], w_enc_codes[:], w_enc_scales[:])
            quantise(nc, w_pred_grouped[:], w_pred_codes[:], w_pred_scales[:])

            for n in range(TOKEN_TILES):
                is_encoder = n * P < ENC_TOKENS
                codes = w_enc_codes if is_encoder else w_pred_codes
                scales = w_enc_scales if is_encoder else w_pred_scales
                bias = b_enc_columns if is_encoder else b_pred_columns
                product = first_psum.tile([P, PACK, P], F32)
                for j in range(PACK):
                    nc.tensor.matmul_mx(
                        out=product[:, j, :],
                        lhsT=codes[:, j * P : (j + 1) * P].bitcast(FP8X4),
                        lhsT_scale=scales[:, j * P : (j + 1) * P],
                        rhs=token_codes[:, n * P : (n + 1) * P].bitcast(FP8X4),
                        rhs_scale=token_scales[:, n * P : (n + 1) * P],
                        start=True,
                        stop=True,
                    )
                nc.vector.tensor_tensor(
                    out=projected[:, n * P : (n + 1) * P, :],
                    in0=product[:].rearrange("p j r -> p r j"),
                    in1=bias.unsqueeze(1).to_broadcast([P, P, PACK]),
                    op=ADD,
                )

            w_out_grouped = keep.tile([P, VOCAB, PACK], BF16, align_bytes=64)
            nc.vector.tensor_copy(
                out=w_out_grouped[:], in_=w_out_raw[:].rearrange("p t c -> p c t")
            )
            quantise(nc, w_out_grouped[:], w_out_codes[:], w_out_scales[:])

        with (
            tc.tile_pool(name="work", bufs=3) as work,
            tc.tile_pool(name="wide", bufs=3) as wide,
            tc.psum_pool(name="psum", bufs=HALF_OF_PSUM) as psum,
        ):
            summed_of = {}
            joint_of = {}
            codes_of = {}
            biased_of = {}
            logits_of = {}

            def form_sum(r):
                b = r * T_STEP // T_LEN
                enc_first = r * T_STEP
                pred_first = ENC_TOKENS + b * U_LEN
                summed_of[r] = work.tile([P, T_STEP, U_LEN, PACK], F32, name="summed")
                for engine, first, last in (
                    (nc.vector, 0, T_ON_VECTOR),
                    (nc.gpsimd, T_ON_VECTOR, T_STEP),
                ):
                    shape = [P, last - first, U_LEN, PACK]
                    engine.tensor_tensor(
                        out=summed_of[r][:, first:last, :, :],
                        in0=projected[:, enc_first + first : enc_first + last, :]
                        .unsqueeze(2)
                        .to_broadcast(shape),
                        in1=projected[:, pred_first : pred_first + U_LEN, :]
                        .unsqueeze(1)
                        .to_broadcast(shape),
                        op=ADD,
                    )

            def take_tanh(r):
                joint_of[r] = work.tile([P, ROUND_ROWS, PACK], BF16, align_bytes=64, name="joint")
                nc.scalar.activation(
                    out=joint_of[r][:],
                    in_=summed_of[r][:].rearrange("p t u j -> p (t u) j"),
                    func=TANH,
                )

            def quantise_joint(r):
                codes = work.tile([P, ROUND_ROWS], U32, align_bytes=64, name="joint_codes")
                scales = work.tile([P, ROUND_ROWS], U8, align_bytes=64, name="joint_scales")
                quantise(nc, joint_of[r][:], codes[:], scales[:])
                codes_of[r] = (codes, scales)

            def project(r, half):
                if half == 0:
                    biased_of[r] = wide.tile([P, VOCAB_BLOCKS, ROUND_ROWS], F32, name="biased")
                codes, scales = codes_of[r]
                blocks = range(half * BLOCKS_IN_BANK, (half + 1) * BLOCKS_IN_BANK)
                products = {}
                for c in blocks:
                    products[c] = psum.tile([P, ROUND_ROWS], F32, name="product")
                    nc.tensor.matmul_mx(
                        out=products[c][:],
                        lhsT=w_out_codes[:, c * P : (c + 1) * P].bitcast(FP8X4),
                        lhsT_scale=w_out_scales[:, c * P : (c + 1) * P],
                        rhs=codes[:].bitcast(FP8X4),
                        rhs_scale=scales[:],
                        start=True,
                        stop=True,
                    )
                for c in blocks:
                    if c < BLOCKS_ON_SCALAR:
                        nc.scalar.activation(
                            out=biased_of[r][:, c, :],
                            in_=products[c][:],
                            func=IDENTITY,
                            bias=b_out_columns[:, c : c + 1],
                        )
                    else:
                        nc.vector.tensor_scalar(
                            out=biased_of[r][:, c, :],
                            in0=products[c][:],
                            scalar1=b_out_columns[:, c : c + 1],
                            scalar2=None,
                            op0=ADD,
                        )

            def turn_back(r, m):
                turned = []
                for h in range(VOCAB_HALVES):
                    bank = psum.tile([P, BLOCKS_IN_BANK, P], F32, name="turned")
                    for i in range(BLOCKS_IN_BANK):
                        nc.tensor.transpose(
                            bank[:, i, :],
                            biased_of[r][:, h * BLOCKS_IN_BANK + i, m * P : (m + 1) * P],
                            identity_f32[:],
                        )
                    turned.append(bank)
                return turned

            def clamp_and_store(r, m, turned):
                if m == 0:
                    logits_of[r] = wide.tile([P, ROW_TILES, VOCAB], F32, name="logits")
                for h in range(VOCAB_HALVES):
                    nc.vector.tensor_scalar(
                        out=logits_of[r][:, m, h * BANK : (h + 1) * BANK],
                        in0=turned[h][:].rearrange("p i v -> p (i v)"),
                        scalar1=LOGIT_CLAMP,
                        scalar2=-LOGIT_CLAMP,
                        op0=MIN,
                        op1=MAX,
                    )
                first_row = r * ROUND_ROWS + m * P
                nc.sync.dma_start(
                    out=out_rows[first_row : first_row + P, :], in_=logits_of[r][:, m, :]
                )

            with tc.manual_schedule():
                for r in range(3):
                    form_sum(r)
                    take_tanh(r)
                quantise_joint(0)
                quantise_joint(1)
                project(0, 0)
                project(0, 1)
                for r in range(ROUNDS):
                    if r + 3 < ROUNDS:
                        form_sum(r + 3)
                    if r + 2 < ROUNDS:
                        quantise_joint(r + 2)
                    for half in range(VOCAB_HALVES):
                        if r + 1 < ROUNDS:
                            project(r + 1, half)
                        if half == 0 and r + 3 < ROUNDS:
                            take_tanh(r + 3)
                        row_tiles = range(half * 2, half * 2 + 2)
                        turned_of = {}
                        for m in row_tiles:
                            turned_of[m] = turn_back(r, m)
                        for m in row_tiles:
                            clamp_and_store(r, m, turned_of[m])
